import numpy as np
import ml_dtypes


def mxq(x, axis, fmt="e4m3"):
    dtype, down = {"e4m3": (ml_dtypes.float8_e4m3fn, 7), "e5m2": (ml_dtypes.float8_e5m2, 14)}[fmt]
    v = np.moveaxis(np.asarray(x, np.float32).astype(ml_dtypes.bfloat16).astype(np.float64), axis, -1)
    blocks = v.reshape(v.shape[:-1] + (-1, 32))
    amax = np.abs(blocks).max(-1, keepdims=True)
    byte = np.maximum(np.where(amax > 0, np.frexp(amax)[1] - 1 + 127, 0) - down, 1)
    scale = np.exp2(byte - 127.0)
    codes = (blocks / scale).astype(np.float32).astype(dtype).astype(np.float64)
    return np.moveaxis((codes * scale).reshape(v.shape), -1, axis)


WIDE = False


def mx_kscale(k):
    if not WIDE:
        return np.ones(k)
    levels = np.array([10, -10, 5, -5, 0])
    a = np.random.permutation(np.resize(levels, k // 512 * 4)).reshape(k // 512, 4)
    idx = np.arange(k)
    return np.exp2(a[idx // 512, idx % 128 // 32])


BF16 = ml_dtypes.bfloat16


def bf(x):
    return np.asarray(x, np.float32).astype(BF16)


def f64(x):
    return np.asarray(x).astype(np.float64)


B, S, DV, D, H, A = 2, 256, 1024, 1024, 8, 64
LN_EPS = 1e-3


def setup_inputs():
    s = mx_kscale(DV)
    return {
        "attn": bf(np.random.standard_normal((B, H, S, DV)) * 0.4 * s),
        "Wo": bf(np.random.standard_normal((H, DV, D)) * 0.6 / np.sqrt(DV * H) / s[None, :, None]),
        "bo": bf(np.random.standard_normal((H, D)) * 0.12 / np.sqrt(H)),
        "query_inputs": bf(np.random.standard_normal((B, S, D)) * 0.1),
        "gamma": bf(1.0 + 0.1 * np.random.standard_normal(D)),
        "beta": bf(0.1 * np.random.standard_normal(D)),
    }


def reference(attn, Wo, bo, query_inputs, gamma, beta):
    pre = mxq(f64(attn), 3, "e4m3") @ mxq(f64(Wo), 1, "e4m3")
    head_out = np.maximum(pre + f64(bo)[None, :, None, :], 0.0)
    x = f64(query_inputs) + head_out.sum(axis=1)
    mean = x.mean(axis=-1, keepdims=True)
    var = x.var(axis=-1, keepdims=True)
    return f64(gamma) * (x - mean) / np.sqrt(var + LN_EPS) + f64(beta)

@@ -1,0 +1,311 @@
+from contextlib import ExitStack
+
+import concourse.mybir as mybir
+from concourse.masks import make_identity
+
+F32 = mybir.dt.float32
+BF16 = mybir.dt.bfloat16
+U32 = mybir.dt.uint32
+U8 = mybir.dt.uint8
+FP8X4 = mybir.dt.float8_e4m3fn_x4
+ALU = mybir.AluOpType
+ACT = mybir.ActivationFunctionType
+
+P = 128
+B, H, S, DV, D = 2, 8, 256, 1024, 1024
+NS = B * S
+G = DV // 512
+DT = D // P
+HALF = D // 2
+UNITS = 2 * H
+LN_EPS = 1e-3
+FLOPS = 2 * B * H * S * DV * D
+
+S_HEADS = (0, 2, 4, 6)
+V_COLS = (320, 320, 512, 512, 320, 320) + (256,) * 10
+G_COLS = (0,) * 16
+
+
+def tile_multiheadattentionunit_pa_kernel(tc, attn, Wo, bo, query_inputs, gamma, beta, out):
+    nc = tc.nc
+    with ExitStack() as ctx:
+        const = ctx.enter_context(tc.tile_pool(name="const", bufs=1))
+        wraw_pool = ctx.enter_context(tc.tile_pool(name="wraw", bufs=3))
+        wgrp_pool = ctx.enter_context(tc.tile_pool(name="wgrp", bufs=3))
+        wq_pool = ctx.enter_context(tc.tile_pool(name="wq", bufs=4))
+        araw_pool = ctx.enter_context(tc.tile_pool(name="araw", bufs=3))
+        agrp_pool = ctx.enter_context(tc.tile_pool(name="agrp", bufs=3))
+        aq_pool = ctx.enter_context(tc.tile_pool(name="aq", bufs=3))
+        small = ctx.enter_context(tc.tile_pool(name="small", bufs=4))
+        ps_xt = ctx.enter_context(tc.psum_pool(name="ps_xt", bufs=2))
+        ps_mm = ctx.enter_context(tc.psum_pool(name="ps_mm", bufs=6))
+        ctx.enter_context(tc.manual_schedule())
+
+        a_raws = {}
+        w_raws = {}
+
+        def load_a(h, src):
+            a_raw = araw_pool.tile([P, 4, DV], BF16, name="a_raw")
+            nc.sync.dma_start(
+                out=a_raw[:].rearrange("p (b t) k -> p b (t k)", b=B),
+                in_=src.rearrange("b (p t) k -> p b (t k)", t=2),
+            )
+            a_raws[h] = a_raw
+
+        def load_w(h):
+            w_raw = wraw_pool.tile([P, 8 * D], BF16, name="w_raw")
+            w_raws[h] = w_raw
+            if h == 0:
+                rows = w_raw[:].rearrange("p (a e d) -> p a e d", a=4, e=2)
+                for dh in range(2):
+                    for a in range(4):
+                        nc.sync.dma_start(
+                            out=rows[:, a, :, dh * HALF : (dh + 1) * HALF],
+                            in_=Wo[h, a * 256 : (a + 1) * 256, dh * HALF : (dh + 1) * HALF].rearrange(
+                                "(p e) d -> p e d", e=2
+                            ),
+                        )
+            else:
+                nc.sync.dma_start(
+                    out=w_raw[:].rearrange("p (a x) -> p a x", a=4),
+                    in_=Wo[h].rearrange("(a p e) d -> p a (e d)", a=4, e=2),
+                )
+
+        for h in range(3):
+            load_a(h, attn[:, h])
+            load_w(h)
+
+        warm = const.tile([P, 1], F32, name="warm")
+        nc.vector.memset(warm[:], 1.0)
+        nc.scalar.activation(out=warm[:], in_=warm[:], func=ACT.Sqrt)
+        ident_f = const.tile([P, P], F32, name="ident_f")
+        make_identity(nc, ident_f[:])
+        ident_b = const.tile([P, P], BF16, name="ident_b")
+        make_identity(nc, ident_b[:])
+        ones_b = const.tile([P, P], BF16, name="ones_b")
+        nc.vector.memset(ones_b[:], 1.0)
+        bo_t = const.tile([P, P], BF16, name="bo_t")
+        nc.vector.memset(bo_t[:], 0.0)
+        nc.scalar.dma_start(out=bo_t[0 : H * DT, :], in_=bo.rearrange("h (t c) -> (h t) c", c=P))
+        bo_pad = const.tile([P, D], BF16, name="bo_pad")
+        nc.vector.memset(bo_pad[:], 0.0)
+        v_heads = [h for h in range(H) if h not in S_HEADS]
+        for r, h in enumerate(v_heads):
+            nc.scalar.dma_start(out=bo_pad[r : r + 1, :], in_=bo[h : h + 1, :])
+        gamma_b = const.tile([P, D], BF16, name="gamma_b")
+        beta_b = const.tile([P, D], BF16, name="beta_b")
+
+        bT_ps = ps_xt.tile([P, P], BF16, name="bT_ps", tag="xt")
+        nc.tensor.transpose(bT_ps[:], bo_t[:], ident_b[:])
+        bpos = const.tile([P, P], F32, name="bpos")
+        nc.vector.tensor_copy(out=bpos[:], in_=bT_ps[:])
+        negb = const.tile([P, P], F32, name="negb")
+        nc.vector.tensor_scalar(out=negb[:], in0=bT_ps[:], scalar1=-1.0, scalar2=None, op0=ALU.mult)
+
+        xts = {}
+        a_grps = {}
+        a_q = {}
+        w_grps = {}
+        w_q = {}
+        pss = {}
+        accs = []
+
+        def in_range(k):
+            return 0 <= k < UNITS
+
+        def pe_transposes(k):
+            h, g = divmod(k, 2)
+            a_raw = a_raws[h]
+            xts[k] = []
+            for half in range(2):
+                xt = ps_xt.tile([P, 2, 256], F32, name="xt", tag="xt")
+                for jj in range(2):
+                    words = a_raw[:, 2 * half + jj, :].bitcast(F32)
+                    for u in range(2):
+                        c0 = 256 * g + 128 * u
+                        nc.tensor.transpose(xt[:, u, jj * P : (jj + 1) * P], words[:, c0 : c0 + P], ident_f[:])
+                xts[k].append(xt)
+
+        def s_exits(k):
+            a_grp = agrp_pool.tile([P, NS * 2], F32, name="a_grp", align_bytes=64)
+            a_grp3 = a_grp[:].rearrange("p (c u) -> p c u", u=2)
+            for half in range(2):
+                nc.scalar.copy(
+                    out=a_grp3[:, half * 256 : (half + 1) * 256, :],
+                    in_=xts[k][half][:].rearrange("p u c -> p c u"),
+                )
+            a_grps[k] = a_grp
+
+        def v_quant_a(k):
+            h, g = divmod(k, 2)
+            if g == 0:
+                a_codes = aq_pool.tile([P, G * NS], U32, name="a_codes", align_bytes=64)
+                a_sc = aq_pool.tile([P, G * NS], U8, name="a_sc", align_bytes=64)
+                a_q[h] = (a_codes, a_sc)
+            a_codes, a_sc = a_q[h]
+            nc.vector.quantize_mx(
+                out=a_codes[:, g * NS : (g + 1) * NS].bitcast(FP8X4),
+                scales=a_sc[:, g * NS : (g + 1) * NS],
+                in_=a_grps[k][:].bitcast(BF16),
+            )
+
+        def v_copy(o, i):
+            nc.vector.tensor_copy(out=o, in_=i)
+
+        def s_copy(o, i):
+            nc.scalar.copy(out=o, in_=i)
+
+        def g_copy(o, i):
+            nc.gpsimd.tensor_scalar(out=o, in0=i, scalar1=1.0, scalar2=0.0, op0=ALU.mult, op1=ALU.add)
+
+        def regroup(n, copy, c0, c1):
+            if c1 <= c0:
+                return
+            h, dh = divmod(n, 2)
+            if n not in w_grps:
+                w_grp_new = wgrp_pool.tile([P, G * HALF * 4], BF16, name="w_grp", tag="w_grp", align_bytes=64)
+                w_grps[n] = w_grp_new
+            dst = w_grps[n][:].rearrange("p (g d t) -> p g d t", g=G, t=4)
+            rows = w_raws[h][:].rearrange("p (r d) -> p r d", r=8)
+            for g in range(G):
+                copy(
+                    dst[:, g, c0:c1, :].rearrange("p (c i) t -> p c t i", i=4),
+                    rows[:, 4 * g : 4 * g + 4, dh * HALF + c0 : dh * HALF + c1].rearrange("p t (c i) -> p c t i", i=4),
+                )
+
+        def v_quant_w(n):
+            w_codes = wq_pool.tile([P, G * HALF], U32, name="w_codes", align_bytes=64)
+            w_sc = wq_pool.tile([P, G * HALF], U8, name="w_sc", align_bytes=64)
+            nc.vector.quantize_mx(out=w_codes[:].bitcast(FP8X4), scales=w_sc[:], in_=w_grps[n][:])
+            w_q[n] = (w_codes, w_sc)
+
+        def pe_mm(n):
+            h, dh = divmod(n, 2)
+            a_codes, a_sc = a_q[h]
+            w_codes, w_sc = w_q[n]
+            pss[n] = []
+            for dd in range(4):
+                ps = ps_mm.tile([P, NS], F32, name="ps", tag="mm")
+                for g in range(G):
+                    w0 = g * HALF + dd * P
+                    nc.tensor.matmul_mx(
+                        out=ps[:],
+                        lhsT=w_codes[:, w0 : w0 + P].bitcast(FP8X4),
+                        lhsT_scale=w_sc[:, w0 : w0 + P],
+                        rhs=a_codes[:, g * NS : (g + 1) * NS].bitcast(FP8X4),
+                        rhs_scale=a_sc[:, g * NS : (g + 1) * NS],
+                        start=(g == 0),
+                        stop=(g == G - 1),
+                    )
+                pss[n].append(ps)
+
+        def take_out(n):
+            h, dh = divmod(n, 2)
+            if h in S_HEADS and dh == 0:
+                acc_new = const.tile([P, DT, NS], F32, name="acc%d" % h)
+                accs.append(acc_new)
+            acc = accs[-1]
+            for dd in range(4):
+                dt = dh * 4 + dd
+                col = h * DT + dt
+                if h in S_HEADS:
+                    nc.scalar.activation(
+                        out=acc[:, dt, :], in_=pss[n][dd][:], func=ACT.Relu, bias=bpos[:, col : col + 1], scale=1.0
+                    )
+                else:
+                    nc.vector.scalar_tensor_tensor(
+                        out=acc[:, dt, :],
+                        in0=pss[n][dd][:],
+                        scalar=negb[:, col : col + 1],
+                        in1=acc[:, dt, :],
+                        op0=ALU.max,
+                        op1=ALU.add,
+                    )
+
+        xps = {}
+
+        def pe_back(j, first_chains):
+            if first_chains:
+                xps[j] = []
+            for hf in range(2):
+                if first_chains:
+                    xp = ps_mm.tile([P, HALF], F32, name="xp", tag="mm")
+                    xps[j].append(xp)
+                    nc.tensor.matmul(
+                        out=xp[:], lhsT=ident_b[:], rhs=a_raws[H][:, j, hf * HALF : (hf + 1) * HALF], start=True, stop=False
+                    )
+                    nc.tensor.matmul(
+                        out=xp[:], lhsT=ones_b[:], rhs=bo_pad[:, hf * HALF : (hf + 1) * HALF], start=False, stop=False
+                    )
+                xp = xps[j][hf]
+                chain_list = accs[:-1] if first_chains else accs[-1:]
+                for acc in chain_list:
+                    for dd in range(4):
+                        nc.tensor.matmul(
+                            out=xp[:, dd * P : (dd + 1) * P],
+                            lhsT=acc[:, hf * 4 + dd, j * P : (j + 1) * P],
+                            rhs=ident_f[:],
+                            is_transpose=True,
+                            start=False,
+                            stop=(not first_chains and dd == 3),
+                        )
+
+        for n in range(-3, UNITS):
+            if in_range(n + 3):
+                pe_transposes(n + 3)
+                s_exits(n + 3)
+            if n == UNITS - 2:
+                pe_back(0, True)
+            if in_range(n):
+                pe_mm(n)
+            if in_range(n + 2):
+                v_quant_a(n + 2)
+            if in_range(n + 1):
+                v_quant_w(n + 1)
+            if in_range(n + 2):
+                m = n + 2
+                regroup(m, v_copy, 0, V_COLS[m])
+                regroup(m, g_copy, V_COLS[m], V_COLS[m] + G_COLS[m])
+                regroup(m, s_copy, V_COLS[m] + G_COLS[m], HALF)
+            if in_range(n):
+                take_out(n)
+            if (n + 7) % 2 == 0:
+                h = (n + 7) // 2
+                if 3 <= h < H:
+                    load_a(h, attn[:, h])
+                    load_w(h)
+                if h == H:
+                    load_a(H, query_inputs)
+                    nc.sync.dma_start(out=gamma_b[:], in_=gamma.partition_broadcast(P))
+                    nc.sync.dma_start(out=beta_b[:], in_=beta.partition_broadcast(P))
+
+        for j in range(4):
+            if j > 0:
+                pe_back(j, True)
+            pe_back(j, False)
+        for j in range(4):
+            stats = small.tile([P, 2, 6], F32, name="stats")
+            for hf in range(2):
+                nc.vector.bn_stats(out=stats[:, hf, :], in_=xps[j][hf][:])
+            mv = small.tile([P, 2], F32, name="mv")
+            nc.vector.bn_aggr(out=mv[:], in_=stats[:].rearrange("p a b -> p (a b)"))
+            ve = small.tile([P, 1], F32, name="ve")
+            nc.vector.tensor_scalar(out=ve[:], in0=mv[:, 1:2], scalar1=LN_EPS, scalar2=None, op0=ALU.add)
+            sd = small.tile([P, 1], F32, name="sd")
+            nc.scalar.activation(out=sd[:], in_=ve[:], func=ACT.Sqrt)
+            to = wgrp_pool.tile([P, 2, D], F32, name="to", tag="w_grp", align_bytes=64)
+            for hf in range(2):
+                nc.vector.scalar_tensor_tensor(
+                    out=to[:, 0, hf * HALF : (hf + 1) * HALF],
+                    in0=xps[j][hf][:],
+                    scalar=mv[:, 0:1],
+                    in1=gamma_b[:, hf * HALF : (hf + 1) * HALF],
+                    op0=ALU.subtract,
+                    op1=ALU.mult,
+                )
+            rstd = small.tile([P, 1], F32, name="rstd")
+            nc.vector.reciprocal(out=rstd[:], in_=sd[:])
+            nc.vector.scalar_tensor_tensor(
+                out=to[:, 1, :], in0=to[:, 0, :], scalar=rstd[:], in1=beta_b[:], op0=ALU.mult, op1=ALU.add
+            )
+            nc.sync.dma_start(out=out[j // 2].rearrange("(p t) d -> p t d", t=2)[:, j % 2, :], in_=to[:, 1, :])

@@ -21,8 +21,8 @@ UNITS = 2 * H
 LN_EPS = 1e-3
 FLOPS = 2 * B * H * S * DV * D
 
-S_HEADS = (0, 2, 4, 6)
-V_COLS = (320, 320, 512, 512, 320, 320) + (256,) * 10
+S_HEADS = (0, 3, 6)
+V_COLS = tuple(512 if n < 4 else (416 if (n - 2) // 2 in S_HEADS else 96) for n in range(16))
 G_COLS = (0,) * 16
 
 
@@ -229,7 +229,10 @@ def tile_multiheadattentionunit_pa_kernel(tc, attn, Wo, bo, query_inputs, gamma,
                 xps[j] = []
             for hf in range(2):
                 if first_chains:
-                    xp = ps_mm.tile([P, HALF], F32, name="xp", tag="mm")
+                    if j == 0:
+                        xp = ps_xt.tile([P, HALF], F32, name="xp0", tag="xt")
+                    else:
+                        xp = ps_mm.tile([P, HALF], F32, name="xp", tag="mm")
                     xps[j].append(xp)
                     nc.tensor.matmul(
                         out=xp[:], lhsT=ident_b[:], rhs=a_raws[H][:, j, hf * HALF : (hf + 1) * HALF], start=True, stop=False
@@ -254,8 +257,10 @@ def tile_multiheadattentionunit_pa_kernel(tc, attn, Wo, bo, query_inputs, gamma,
             if in_range(n + 3):
                 pe_transposes(n + 3)
                 s_exits(n + 3)
-            if n == UNITS - 2:
+            if n == UNITS - 3:
                 pe_back(0, True)
+            if n == UNITS - 2:
+                pe_back(1, True)
             if in_range(n):
                 pe_mm(n)
             if in_range(n + 2):
@@ -280,7 +285,7 @@ def tile_multiheadattentionunit_pa_kernel(tc, attn, Wo, bo, query_inputs, gamma,
                     nc.sync.dma_start(out=beta_b[:], in_=beta.partition_broadcast(P))
 
         for j in range(4):
-            if j > 0:
+            if j > 1:
                 pe_back(j, True)
             pe_back(j, False)
         for j in range(4):
@@ -305,7 +310,11 @@ def tile_multiheadattentionunit_pa_kernel(tc, attn, Wo, bo, query_inputs, gamma,
                 )
             rstd = small.tile([P, 1], F32, name="rstd")
             nc.vector.reciprocal(out=rstd[:], in_=sd[:])
-            nc.vector.scalar_tensor_tensor(
-                out=to[:, 1, :], in0=to[:, 0, :], scalar=rstd[:], in1=beta_b[:], op0=ALU.mult, op1=ALU.add
-            )
+            if j == 3:
+                nc.vector.scalar_tensor_tensor(
+                    out=to[:, 1, :], in0=to[:, 0, :], scalar=rstd[:], in1=beta_b[:], op0=ALU.mult, op1=ALU.add
+                )
+            else:
+                nc.scalar.activation(out=to[:, 1, :], in_=to[:, 0, :], func=ACT.Copy, scale=rstd[:])
+                nc.gpsimd.tensor_tensor(out=to[:, 1, :], in0=to[:, 1, :], in1=beta_b[:], op=ALU.add)
             nc.sync.dma_start(out=out[j // 2].rearrange("(p t) d -> p t d", t=2)[:, j % 2, :], in_=to[:, 1, :])

@@ -21,9 +21,8 @@ UNITS = 2 * H
 LN_EPS = 1e-3
 FLOPS = 2 * B * H * S * DV * D
 
-S_HEADS = (0, 3, 6)
-V_COLS = tuple(512 if n < 4 else (416 if (n - 2) // 2 in S_HEADS else 96) for n in range(16))
-G_COLS = (0,) * 16
+S_HEADS = (0, 2, 4, 7)
+MAIN = 384
 
 
 def tile_multiheadattentionunit_pa_kernel(tc, attn, Wo, bo, query_inputs, gamma, beta, out):
@@ -32,6 +31,7 @@ def tile_multiheadattentionunit_pa_kernel(tc, attn, Wo, bo, query_inputs, gamma,
         const = ctx.enter_context(tc.tile_pool(name="const", bufs=1))
         wraw_pool = ctx.enter_context(tc.tile_pool(name="wraw", bufs=3))
         wgrp_pool = ctx.enter_context(tc.tile_pool(name="wgrp", bufs=3))
+        wlast_pool = ctx.enter_context(tc.tile_pool(name="wlast", bufs=1))
         wq_pool = ctx.enter_context(tc.tile_pool(name="wq", bufs=4))
         araw_pool = ctx.enter_context(tc.tile_pool(name="araw", bufs=3))
         agrp_pool = ctx.enter_context(tc.tile_pool(name="agrp", bufs=3))
@@ -106,6 +106,7 @@ def tile_multiheadattentionunit_pa_kernel(tc, attn, Wo, bo, query_inputs, gamma,
         a_grps = {}
         a_q = {}
         w_grps = {}
+        w_lasts = {}
         w_q = {}
         pss = {}
         accs = []
@@ -162,21 +163,32 @@ def tile_multiheadattentionunit_pa_kernel(tc, attn, Wo, bo, query_inputs, gamma,
             if c1 <= c0:
                 return
             h, dh = divmod(n, 2)
-            if n not in w_grps:
-                w_grp_new = wgrp_pool.tile([P, G * HALF * 4], BF16, name="w_grp", tag="w_grp", align_bytes=64)
-                w_grps[n] = w_grp_new
-            dst = w_grps[n][:].rearrange("p (g d t) -> p g d t", g=G, t=4)
+            if c0 < MAIN:
+                if n not in w_grps:
+                    w_grp_new = wgrp_pool.tile([P, G * MAIN * 4], BF16, name="w_grp", tag="w_grp", align_bytes=64)
+                    w_grps[n] = w_grp_new
+                dst = w_grps[n][:].rearrange("p (g d t) -> p g d t", g=G, t=4)[:, :, c0:c1, :]
+            else:
+                w_last_new = wlast_pool.tile([P, G * P * 4], BF16, name="w_last", align_bytes=64)
+                w_lasts[n] = w_last_new
+                dst = w_last_new[:].rearrange("p (g d t) -> p g d t", g=G, t=4)
             rows = w_raws[h][:].rearrange("p (r d) -> p r d", r=8)
             for g in range(G):
                 copy(
-                    dst[:, g, c0:c1, :].rearrange("p (c i) t -> p c t i", i=4),
+                    dst[:, g, :, :].rearrange("p (c i) t -> p c t i", i=4),
                     rows[:, 4 * g : 4 * g + 4, dh * HALF + c0 : dh * HALF + c1].rearrange("p t (c i) -> p c t i", i=4),
                 )
 
         def v_quant_w(n):
             w_codes = wq_pool.tile([P, G * HALF], U32, name="w_codes", align_bytes=64)
             w_sc = wq_pool.tile([P, G * HALF], U8, name="w_sc", align_bytes=64)
-            nc.vector.quantize_mx(out=w_codes[:].bitcast(FP8X4), scales=w_sc[:], in_=w_grps[n][:])
+            for src, e0, e1, word0 in ((w_grps[n], 0, 2048, 0), (w_grps[n], 2048, 3072, 512), (w_lasts[n], 0, 1024, 768)):
+                words = (e1 - e0) // 4
+                nc.vector.quantize_mx(
+                    out=w_codes[:, word0 : word0 + words].bitcast(FP8X4),
+                    scales=w_sc[:, word0 : word0 + words],
+                    in_=src[:, e0:e1],
+                )
             w_q[n] = (w_codes, w_sc)
 
         def pe_mm(n):
@@ -187,7 +199,7 @@ def tile_multiheadattentionunit_pa_kernel(tc, attn, Wo, bo, query_inputs, gamma,
             for dd in range(4):
                 ps = ps_mm.tile([P, NS], F32, name="ps", tag="mm")
                 for g in range(G):
-                    w0 = g * HALF + dd * P
+                    w0 = g * MAIN + dd * P if dd < 3 else 2 * MAIN + g * P
                     nc.tensor.matmul_mx(
                         out=ps[:],
                         lhsT=w_codes[:, w0 : w0 + P].bitcast(FP8X4),
@@ -224,11 +236,12 @@ def tile_multiheadattentionunit_pa_kernel(tc, attn, Wo, bo, query_inputs, gamma,
 
         xps = {}
 
-        def pe_back(j, first_chains):
-            if first_chains:
+        def pe_back(j, sums):
+            opening = 0 in sums
+            if opening:
                 xps[j] = []
             for hf in range(2):
-                if first_chains:
+                if opening:
                     if j == 0:
                         xp = ps_xt.tile([P, HALF], F32, name="xp0", tag="xt")
                     else:
@@ -241,16 +254,15 @@ def tile_multiheadattentionunit_pa_kernel(tc, attn, Wo, bo, query_inputs, gamma,
                         out=xp[:], lhsT=ones_b[:], rhs=bo_pad[:, hf * HALF : (hf + 1) * HALF], start=False, stop=False
                     )
                 xp = xps[j][hf]
-                chain_list = accs[:-1] if first_chains else accs[-1:]
-                for acc in chain_list:
+                for ci in sums:
                     for dd in range(4):
                         nc.tensor.matmul(
                             out=xp[:, dd * P : (dd + 1) * P],
-                            lhsT=acc[:, hf * 4 + dd, j * P : (j + 1) * P],
+                            lhsT=accs[ci][:, hf * 4 + dd, j * P : (j + 1) * P],
                             rhs=ident_f[:],
                             is_transpose=True,
                             start=False,
-                            stop=(not first_chains and dd == 3),
+                            stop=(ci == len(S_HEADS) - 1 and dd == 3),
                         )
 
         for n in range(-3, UNITS):
@@ -258,20 +270,22 @@ def tile_multiheadattentionunit_pa_kernel(tc, attn, Wo, bo, query_inputs, gamma,
                 pe_transposes(n + 3)
                 s_exits(n + 3)
             if n == UNITS - 3:
-                pe_back(0, True)
+                pe_back(0, (0, 1))
             if n == UNITS - 2:
-                pe_back(1, True)
+                pe_back(1, (0, 1))
+            if n == UNITS - 1:
+                pe_back(0, (2,))
+                pe_back(1, (2,))
             if in_range(n):
                 pe_mm(n)
+            vector_empties = in_range(n) and n // 2 not in S_HEADS
             if in_range(n + 2):
+                regroup(n + 2, s_copy if vector_empties else v_copy, 0, MAIN)
                 v_quant_a(n + 2)
             if in_range(n + 1):
                 v_quant_w(n + 1)
             if in_range(n + 2):
-                m = n + 2
-                regroup(m, v_copy, 0, V_COLS[m])
-                regroup(m, g_copy, V_COLS[m], V_COLS[m] + G_COLS[m])
-                regroup(m, s_copy, V_COLS[m] + G_COLS[m], HALF)
+                regroup(n + 2, g_copy if vector_empties else v_copy, MAIN, HALF)
             if in_range(n):
                 take_out(n)
             if (n + 7) % 2 == 0:
@@ -285,9 +299,7 @@ def tile_multiheadattentionunit_pa_kernel(tc, attn, Wo, bo, query_inputs, gamma,
                     nc.sync.dma_start(out=beta_b[:], in_=beta.partition_broadcast(P))
 
         for j in range(4):
-            if j > 1:
-                pe_back(j, True)
-            pe_back(j, False)
+            pe_back(j, (3,) if j < 2 else (0, 1, 2, 3))
         for j in range(4):
             stats = small.tile([P, 2, 6], F32, name="stats")
             for hf in range(2):

@@ -39,7 +39,6 @@ def tile_multiheadattentionunit_pa_kernel(tc, attn, Wo, bo, query_inputs, gamma,
         small = ctx.enter_context(tc.tile_pool(name="small", bufs=4))
         ps_xt = ctx.enter_context(tc.psum_pool(name="ps_xt", bufs=2))
         ps_mm = ctx.enter_context(tc.psum_pool(name="ps_mm", bufs=6))
-        ctx.enter_context(tc.manual_schedule())
 
         a_raws = {}
         w_raws = {}

@@ -39,6 +39,7 @@ def tile_multiheadattentionunit_pa_kernel(tc, attn, Wo, bo, query_inputs, gamma,
         small = ctx.enter_context(tc.tile_pool(name="small", bufs=4))
         ps_xt = ctx.enter_context(tc.psum_pool(name="ps_xt", bufs=2))
         ps_mm = ctx.enter_context(tc.psum_pool(name="ps_mm", bufs=6))
+        ctx.enter_context(tc.manual_schedule())
 
         a_raws = {}
         w_raws = {}
@@ -247,13 +248,18 @@ def tile_multiheadattentionunit_pa_kernel(tc, attn, Wo, bo, query_inputs, gamma,
                         xp = ps_mm.tile([P, HALF], F32, name="xp", tag="mm")
                     xps[j].append(xp)
                     nc.tensor.matmul(
-                        out=xp[:], lhsT=ident_b[:], rhs=a_raws[H][:, j, hf * HALF : (hf + 1) * HALF], start=True, stop=False
-                    )
-                    nc.tensor.matmul(
-                        out=xp[:], lhsT=ones_b[:], rhs=bo_pad[:, hf * HALF : (hf + 1) * HALF], start=False, stop=False
+                        out=xp[:], lhsT=ones_b[:], rhs=bo_pad[:, hf * HALF : (hf + 1) * HALF], start=True, stop=False
                     )
                 xp = xps[j][hf]
                 for ci in sums:
+                    if ci == len(S_HEADS) - 1:
+                        nc.tensor.matmul(
+                            out=xp[:],
+                            lhsT=ident_b[:],
+                            rhs=a_raws[H][:, j, hf * HALF : (hf + 1) * HALF],
+                            start=False,
+                            stop=False,
+                        )
                     for dd in range(4):
                         nc.tensor.matmul(
                             out=xp[:, dd * P : (dd + 1) * P],

from contextlib import ExitStack

import concourse.mybir as mybir
from concourse.masks import make_identity

F32 = mybir.dt.float32
BF16 = mybir.dt.bfloat16
U32 = mybir.dt.uint32
U8 = mybir.dt.uint8
FP8X4 = mybir.dt.float8_e4m3fn_x4
ALU = mybir.AluOpType
ACT = mybir.ActivationFunctionType

P = 128
B, H, S, DV, D = 2, 8, 256, 1024, 1024
NS = B * S
G = DV // 512
DT = D // P
HALF = D // 2
UNITS = 2 * H
LN_EPS = 1e-3
FLOPS = 2 * B * H * S * DV * D

S_HEADS = (0, 2, 4, 7)
MAIN = 384


def tile_multiheadattentionunit_pa_kernel(tc, attn, Wo, bo, query_inputs, gamma, beta, out):
    nc = tc.nc
    with ExitStack() as ctx:
        const = ctx.enter_context(tc.tile_pool(name="const", bufs=1))
        wraw_pool = ctx.enter_context(tc.tile_pool(name="wraw", bufs=3))
        wgrp_pool = ctx.enter_context(tc.tile_pool(name="wgrp", bufs=3))
        wlast_pool = ctx.enter_context(tc.tile_pool(name="wlast", bufs=1))
        wq_pool = ctx.enter_context(tc.tile_pool(name="wq", bufs=4))
        araw_pool = ctx.enter_context(tc.tile_pool(name="araw", bufs=3))
        agrp_pool = ctx.enter_context(tc.tile_pool(name="agrp", bufs=3))
        aq_pool = ctx.enter_context(tc.tile_pool(name="aq", bufs=3))
        small = ctx.enter_context(tc.tile_pool(name="small", bufs=4))
        ps_xt = ctx.enter_context(tc.psum_pool(name="ps_xt", bufs=2))
        ps_mm = ctx.enter_context(tc.psum_pool(name="ps_mm", bufs=6))
        ctx.enter_context(tc.manual_schedule())

        a_raws = {}
        w_raws = {}

        def load_a(h, src):
            a_raw = araw_pool.tile([P, 4, DV], BF16, name="a_raw")
            nc.sync.dma_start(
                out=a_raw[:].rearrange("p (b t) k -> p b (t k)", b=B),
                in_=src.rearrange("b (p t) k -> p b (t k)", t=2),
            )
            a_raws[h] = a_raw

        def load_w(h):
            w_raw = wraw_pool.tile([P, 8 * D], BF16, name="w_raw")
            w_raws[h] = w_raw
            if h == 0:
                rows = w_raw[:].rearrange("p (a e d) -> p a e d", a=4, e=2)
                for dh in range(2):
                    for a in range(4):
                        nc.sync.dma_start(
                            out=rows[:, a, :, dh * HALF : (dh + 1) * HALF],
                            in_=Wo[h, a * 256 : (a + 1) * 256, dh * HALF : (dh + 1) * HALF].rearrange(
                                "(p e) d -> p e d", e=2
                            ),
                        )
            else:
                nc.sync.dma_start(
                    out=w_raw[:].rearrange("p (a x) -> p a x", a=4),
                    in_=Wo[h].rearrange("(a p e) d -> p a (e d)", a=4, e=2),
                )

        for h in range(3):
            load_a(h, attn[:, h])
            load_w(h)

        warm = const.tile([P, 1], F32, name="warm")
        nc.vector.memset(warm[:], 1.0)
        nc.scalar.activation(out=warm[:], in_=warm[:], func=ACT.Sqrt)
        ident_f = const.tile([P, P], F32, name="ident_f")
        make_identity(nc, ident_f[:])
        ident_b = const.tile([P, P], BF16, name="ident_b")
        make_identity(nc, ident_b[:])
        ones_b = const.tile([P, P], BF16, name="ones_b")
        nc.vector.memset(ones_b[:], 1.0)
        bo_t = const.tile([P, P], BF16, name="bo_t")
        nc.vector.memset(bo_t[:], 0.0)
        nc.scalar.dma_start(out=bo_t[0 : H * DT, :], in_=bo.rearrange("h (t c) -> (h t) c", c=P))
        bo_pad = const.tile([P, D], BF16, name="bo_pad")
        nc.vector.memset(bo_pad[:], 0.0)
        v_heads = [h for h in range(H) if h not in S_HEADS]
        for r, h in enumerate(v_heads):
            nc.scalar.dma_start(out=bo_pad[r : r + 1, :], in_=bo[h : h + 1, :])
        gamma_b = const.tile([P, D], BF16, name="gamma_b")
        beta_b = const.tile([P, D], BF16, name="beta_b")

        bT_ps = ps_xt.tile([P, P], BF16, name="bT_ps", tag="xt")
        nc.tensor.transpose(bT_ps[:], bo_t[:], ident_b[:])
        bpos = const.tile([P, P], F32, name="bpos")
        nc.vector.tensor_copy(out=bpos[:], in_=bT_ps[:])
        negb = const.tile([P, P], F32, name="negb")
        nc.vector.tensor_scalar(out=negb[:], in0=bT_ps[:], scalar1=-1.0, scalar2=None, op0=ALU.mult)

        xts = {}
        a_grps = {}
        a_q = {}
        w_grps = {}
        w_lasts = {}
        w_q = {}
        pss = {}
        accs = []

        def in_range(k):
            return 0 <= k < UNITS

        def pe_transposes(k):
            h, g = divmod(k, 2)
            a_raw = a_raws[h]
            xts[k] = []
            for half in range(2):
                xt = ps_xt.tile([P, 2, 256], F32, name="xt", tag="xt")
                for jj in range(2):
                    words = a_raw[:, 2 * half + jj, :].bitcast(F32)
                    for u in range(2):
                        c0 = 256 * g + 128 * u
                        nc.tensor.transpose(xt[:, u, jj * P : (jj + 1) * P], words[:, c0 : c0 + P], ident_f[:])
                xts[k].append(xt)

        def s_exits(k):
            a_grp = agrp_pool.tile([P, NS * 2], F32, name="a_grp", align_bytes=64)
            a_grp3 = a_grp[:].rearrange("p (c u) -> p c u", u=2)
            for half in range(2):
                nc.scalar.copy(
                    out=a_grp3[:, half * 256 : (half + 1) * 256, :],
                    in_=xts[k][half][:].rearrange("p u c -> p c u"),
                )
            a_grps[k] = a_grp

        def v_quant_a(k):
            h, g = divmod(k, 2)
            if g == 0:
                a_codes = aq_pool.tile([P, G * NS], U32, name="a_codes", align_bytes=64)
                a_sc = aq_pool.tile([P, G * NS], U8, name="a_sc", align_bytes=64)
                a_q[h] = (a_codes, a_sc)
            a_codes, a_sc = a_q[h]
            nc.vector.quantize_mx(
                out=a_codes[:, g * NS : (g + 1) * NS].bitcast(FP8X4),
                scales=a_sc[:, g * NS : (g + 1) * NS],
                in_=a_grps[k][:].bitcast(BF16),
            )

        def v_copy(o, i):
            nc.vector.tensor_copy(out=o, in_=i)

        def s_copy(o, i):
            nc.scalar.copy(out=o, in_=i)

        def g_copy(o, i):
            nc.gpsimd.tensor_scalar(out=o, in0=i, scalar1=1.0, scalar2=0.0, op0=ALU.mult, op1=ALU.add)

        def regroup(n, copy, c0, c1):
            if c1 <= c0:
                return
            h, dh = divmod(n, 2)
            if c0 < MAIN:
                if n not in w_grps:
                    w_grp_new = wgrp_pool.tile([P, G * MAIN * 4], BF16, name="w_grp", tag="w_grp", align_bytes=64)
                    w_grps[n] = w_grp_new
                dst = w_grps[n][:].rearrange("p (g d t) -> p g d t", g=G, t=4)[:, :, c0:c1, :]
            else:
                w_last_new = wlast_pool.tile([P, G * P * 4], BF16, name="w_last", align_bytes=64)
                w_lasts[n] = w_last_new
                dst = w_last_new[:].rearrange("p (g d t) -> p g d t", g=G, t=4)
            rows = w_raws[h][:].rearrange("p (r d) -> p r d", r=8)
            for g in range(G):
                copy(
                    dst[:, g, :, :].rearrange("p (c i) t -> p c t i", i=4),
                    rows[:, 4 * g : 4 * g + 4, dh * HALF + c0 : dh * HALF + c1].rearrange("p t (c i) -> p c t i", i=4),
                )

        def v_quant_w(n):
            w_codes = wq_pool.tile([P, G * HALF], U32, name="w_codes", align_bytes=64)
            w_sc = wq_pool.tile([P, G * HALF], U8, name="w_sc", align_bytes=64)
            for src, e0, e1, word0 in ((w_grps[n], 0, 2048, 0), (w_grps[n], 2048, 3072, 512), (w_lasts[n], 0, 1024, 768)):
                words = (e1 - e0) // 4
                nc.vector.quantize_mx(
                    out=w_codes[:, word0 : word0 + words].bitcast(FP8X4),
                    scales=w_sc[:, word0 : word0 + words],
                    in_=src[:, e0:e1],
                )
            w_q[n] = (w_codes, w_sc)

        def pe_mm(n):
            h, dh = divmod(n, 2)
            a_codes, a_sc = a_q[h]
            w_codes, w_sc = w_q[n]
            pss[n] = []
            for dd in range(4):
                ps = ps_mm.tile([P, NS], F32, name="ps", tag="mm")
                for g in range(G):
                    w0 = g * MAIN + dd * P if dd < 3 else 2 * MAIN + g * P
                    nc.tensor.matmul_mx(
                        out=ps[:],
                        lhsT=w_codes[:, w0 : w0 + P].bitcast(FP8X4),
                        lhsT_scale=w_sc[:, w0 : w0 + P],
                        rhs=a_codes[:, g * NS : (g + 1) * NS].bitcast(FP8X4),
                        rhs_scale=a_sc[:, g * NS : (g + 1) * NS],
                        start=(g == 0),
                        stop=(g == G - 1),
                    )
                pss[n].append(ps)

        def take_out(n):
            h, dh = divmod(n, 2)
            if h in S_HEADS and dh == 0:
                acc_new = const.tile([P, DT, NS], F32, name="acc%d" % h)
                accs.append(acc_new)
            acc = accs[-1]
            for dd in range(4):
                dt = dh * 4 + dd
                col = h * DT + dt
                if h in S_HEADS:
                    nc.scalar.activation(
                        out=acc[:, dt, :], in_=pss[n][dd][:], func=ACT.Relu, bias=bpos[:, col : col + 1], scale=1.0
                    )
                else:
                    nc.vector.scalar_tensor_tensor(
                        out=acc[:, dt, :],
                        in0=pss[n][dd][:],
                        scalar=negb[:, col : col + 1],
                        in1=acc[:, dt, :],
                        op0=ALU.max,
                        op1=ALU.add,
                    )

        xps = {}

        def pe_back(j, sums):
            opening = 0 in sums
            if opening:
                xps[j] = []
            for hf in range(2):
                if opening:
                    if j == 0:
                        xp = ps_xt.tile([P, HALF], F32, name="xp0", tag="xt")
                    else:
                        xp = ps_mm.tile([P, HALF], F32, name="xp", tag="mm")
                    xps[j].append(xp)
                    nc.tensor.matmul(
                        out=xp[:], lhsT=ones_b[:], rhs=bo_pad[:, hf * HALF : (hf + 1) * HALF], start=True, stop=False
                    )
                xp = xps[j][hf]
                for ci in sums:
                    if ci == len(S_HEADS) - 1:
                        nc.tensor.matmul(
                            out=xp[:],
                            lhsT=ident_b[:],
                            rhs=a_raws[H][:, j, hf * HALF : (hf + 1) * HALF],
                            start=False,
                            stop=False,
                        )
                    for dd in range(4):
                        nc.tensor.matmul(
                            out=xp[:, dd * P : (dd + 1) * P],
                            lhsT=accs[ci][:, hf * 4 + dd, j * P : (j + 1) * P],
                            rhs=ident_f[:],
                            is_transpose=True,
                            start=False,
                            stop=(ci == len(S_HEADS) - 1 and dd == 3),
                        )

        for n in range(-3, UNITS):
            if in_range(n + 3):
                pe_transposes(n + 3)
                s_exits(n + 3)
            if n == UNITS - 3:
                pe_back(0, (0, 1))
            if n == UNITS - 2:
                pe_back(1, (0, 1))
            if n == UNITS - 1:
                pe_back(0, (2,))
                pe_back(1, (2,))
            if in_range(n):
                pe_mm(n)
            vector_empties = in_range(n) and n // 2 not in S_HEADS
            if in_range(n + 2):
                regroup(n + 2, s_copy if vector_empties else v_copy, 0, MAIN)
                v_quant_a(n + 2)
            if in_range(n + 1):
                v_quant_w(n + 1)
            if in_range(n + 2):
                regroup(n + 2, g_copy if vector_empties else v_copy, MAIN, HALF)
            if in_range(n):
                take_out(n)
            if (n + 7) % 2 == 0:
                h = (n + 7) // 2
                if 3 <= h < H:
                    load_a(h, attn[:, h])
                    load_w(h)
                if h == H:
                    load_a(H, query_inputs)
                    nc.sync.dma_start(out=gamma_b[:], in_=gamma.partition_broadcast(P))
                    nc.sync.dma_start(out=beta_b[:], in_=beta.partition_broadcast(P))

        for j in range(4):
            pe_back(j, (3,) if j < 2 else (0, 1, 2, 3))
        for j in range(4):
            stats = small.tile([P, 2, 6], F32, name="stats")
            for hf in range(2):
                nc.vector.bn_stats(out=stats[:, hf, :], in_=xps[j][hf][:])
            mv = small.tile([P, 2], F32, name="mv")
            nc.vector.bn_aggr(out=mv[:], in_=stats[:].rearrange("p a b -> p (a b)"))
            ve = small.tile([P, 1], F32, name="ve")
            nc.vector.tensor_scalar(out=ve[:], in0=mv[:, 1:2], scalar1=LN_EPS, scalar2=None, op0=ALU.add)
            sd = small.tile([P, 1], F32, name="sd")
            nc.scalar.activation(out=sd[:], in_=ve[:], func=ACT.Sqrt)
            to = wgrp_pool.tile([P, 2, D], F32, name="to", tag="w_grp", align_bytes=64)
            for hf in range(2):
                nc.vector.scalar_tensor_tensor(
                    out=to[:, 0, hf * HALF : (hf + 1) * HALF],
                    in0=xps[j][hf][:],
                    scalar=mv[:, 0:1],
                    in1=gamma_b[:, hf * HALF : (hf + 1) * HALF],
                    op0=ALU.subtract,
                    op1=ALU.mult,
                )
            rstd = small.tile([P, 1], F32, name="rstd")
            nc.vector.reciprocal(out=rstd[:], in_=sd[:])
            if j == 3:
                nc.vector.scalar_tensor_tensor(
                    out=to[:, 1, :], in0=to[:, 0, :], scalar=rstd[:], in1=beta_b[:], op0=ALU.mult, op1=ALU.add
                )
            else:
                nc.scalar.activation(out=to[:, 1, :], in_=to[:, 0, :], func=ACT.Copy, scale=rstd[:])
                nc.gpsimd.tensor_tensor(out=to[:, 1, :], in0=to[:, 1, :], in1=beta_b[:], op=ALU.add)
            nc.sync.dma_start(out=out[j // 2].rearrange("(p t) d -> p t d", t=2)[:, j % 2, :], in_=to[:, 1, :])
